import numpy as np
import ml_dtypes


def mxq(x, axis, fmt="e4m3"):
    dtype, down = {"e4m3": (ml_dtypes.float8_e4m3fn, 7), "e5m2": (ml_dtypes.float8_e5m2, 14)}[fmt]
    v = np.moveaxis(np.asarray(x, np.float32).astype(ml_dtypes.bfloat16).astype(np.float64), axis, -1)
    blocks = v.reshape(v.shape[:-1] + (-1, 32))
    amax = np.abs(blocks).max(-1, keepdims=True)
    byte = np.maximum(np.where(amax > 0, np.frexp(amax)[1] - 1 + 127, 0) - down, 1)
    scale = np.exp2(byte - 127.0)
    codes = (blocks / scale).astype(np.float32).astype(dtype).astype(np.float64)
    return np.moveaxis((codes * scale).reshape(v.shape), -1, axis)


WIDE = False


def mx_kscale(k):
    if not WIDE:
        return np.ones(k)
    levels = np.array([10, -10, 5, -5, 0])
    if k % 512:
        return np.exp2(np.random.permutation(np.resize(levels, k // 32))).repeat(32)
    a = np.empty((k // 512, 16))
    for p in range(k // 512):
        a[p, :8] = np.random.permutation(np.resize(levels, 8))
        for g in range(8):
            far = levels[np.abs(levels - a[p, g]) >= 10]
            a[p, g + 8] = far[np.random.randint(len(far))]
    return np.exp2(a.ravel()).repeat(32)


BF16 = ml_dtypes.bfloat16


def bf(x):
    return np.asarray(x, np.float32).astype(BF16)


def f64(x):
    return np.asarray(x).astype(np.float64)


B, S, D, H, QL, KL, ND, VD, RD = 4, 256, 2048, 16, 512, 512, 128, 128, 128
QH = ND + RD
BASE = 10000.0


def rope(v):
    d = v.shape[-1]
    inv_freq = BASE ** (-np.arange(0, d, 2) / d)
    ang = np.arange(v.shape[1])[:, None] * inv_freq[None, :]
    cos = np.cos(ang)[None, :, None, :]
    sin = np.sin(ang)[None, :, None, :]
    v1 = v[..., 0::2]
    v2 = v[..., 1::2]
    o1 = v1 * cos - v2 * sin
    o2 = v1 * sin + v2 * cos
    return np.stack([o1, o2], axis=-1).reshape(v.shape)


def setup_inputs():
    s, t = mx_kscale(D), mx_kscale(QL)
    return {"x": bf(np.random.standard_normal((B, S, D)) * s),
            "Wqa": bf(np.random.standard_normal((D, QL)) / np.sqrt(D) / s[:, None] * t),
            "Wqb": bf(np.random.standard_normal((QL, H * QH)) / np.sqrt(QL) / t[:, None])}


def reference(x, Wqa, Wqb):
    cq = mxq(f64(x), 2, "e4m3") @ mxq(f64(Wqa), 0, "e4m3")
    q = (mxq(cq, 2, "e4m3") @ mxq(f64(Wqb), 0, "e4m3")).reshape(B, S, H, QH)
    q_nope, q_pe = q[..., :ND], q[..., ND:]
    return np.concatenate([q_nope, rope(q_pe)], axis=-1)

@@ -1,0 +1,362 @@
+import math
+from contextlib import ExitStack
+
+import concourse.mybir as mybir
+from concourse.masks import make_identity
+
+F32 = mybir.dt.float32
+BF16 = mybir.dt.bfloat16
+I32 = mybir.dt.int32
+U32 = mybir.dt.uint32
+U8 = mybir.dt.uint8
+FP8X4 = mybir.dt.float8_e4m3fn_x4
+ALU = mybir.AluOpType
+ACT = mybir.ActivationFunctionType
+
+P = 128
+PACK = 4
+K_PASS = P * PACK
+
+BATCH, SEQ, D_MODEL, HEADS, Q_RANK = 4, 256, 2048, 16, 512
+PLAIN, ROTARY = 128, 128
+HEAD = PLAIN + ROTARY
+PAIRS = ROTARY // 2
+PAIR_BITS = 6
+assert 2**PAIR_BITS == PAIRS
+ROPE_BASE = 10000.0
+
+TOKENS = BATCH * SEQ
+TOKEN_TILES = TOKENS // P
+SEQ_HALVES = SEQ // P
+D_PASSES = D_MODEL // K_PASS
+RANK_TILES = Q_RANK // P
+
+CHUNK_HEADS = 4
+CHUNKS = HEADS // CHUNK_HEADS
+CHUNK_COLS = CHUNK_HEADS * HEAD
+BANK = CHUNK_HEADS * PLAIN
+CHUNK_PAIRS = CHUNK_HEADS * PAIRS
+KINDS = 2
+PLAIN_KIND, ROTARY_KIND = 0, 1
+
+LAG = 2
+CHUNK_LAG = 3
+PREPARE_STEPS = 4
+VECTOR_CHUNKS = 2
+VECTOR_ADDS = 4
+PSUM_BANKS = 8
+
+FLOPS = 2 * TOKENS * D_MODEL * Q_RANK + 2 * TOKENS * Q_RANK * HEADS * HEAD
+
+TWO_PI = 2.0 * math.pi
+TWO_PI_HIGH = round(TWO_PI * 2.0**15) / 2.0**15
+TWO_PI_LOW = TWO_PI - TWO_PI_HIGH
+ROUND_MAGIC = 1.5 * 2.0**23
+
+
+def build_rotation_tables(nc, pool):
+    position_int = pool.tile([P, SEQ_HALVES], I32, name="position_int")
+    nc.gpsimd.iota(position_int[:], pattern=[[P, SEQ_HALVES]], base=0, channel_multiplier=1)
+    position = pool.tile([P, SEQ_HALVES], F32, name="position")
+    nc.vector.tensor_copy(out=position[:], in_=position_int[:])
+
+    ratio = ROPE_BASE ** (-2.0 / ROTARY)
+    frequency = pool.tile([P, PAIRS], F32, name="frequency")
+    nc.vector.memset(frequency[:, 0:1], 1.0)
+    for doubling in range(PAIR_BITS):
+        filled = 2**doubling
+        nc.vector.tensor_scalar_mul(
+            out=frequency[:, filled : 2 * filled], in0=frequency[:, 0:filled], scalar1=ratio**filled
+        )
+
+    angle = pool.tile([P, SEQ_HALVES, PAIRS], F32, name="angle")
+    for half in range(SEQ_HALVES):
+        nc.vector.tensor_scalar_mul(
+            out=angle[:, half, :], in0=frequency[:], scalar1=position[:, half : half + 1]
+        )
+
+    turns = pool.tile([P, SEQ_HALVES, PAIRS], F32, name="turns")
+    nc.vector.tensor_scalar(
+        out=turns[:], in0=angle[:], scalar1=1.0 / TWO_PI, scalar2=ROUND_MAGIC, op0=ALU.mult, op1=ALU.add
+    )
+    nc.vector.tensor_scalar_sub(out=turns[:], in0=turns[:], scalar1=ROUND_MAGIC)
+    partly = pool.tile([P, SEQ_HALVES, PAIRS], F32, name="partly")
+    nc.vector.scalar_tensor_tensor(
+        out=partly[:], in0=turns[:], scalar=-TWO_PI_HIGH, in1=angle[:], op0=ALU.mult, op1=ALU.add
+    )
+    reduced = pool.tile([P, SEQ_HALVES, PAIRS], F32, name="reduced")
+    nc.vector.scalar_tensor_tensor(
+        out=reduced[:], in0=turns[:], scalar=-TWO_PI_LOW, in1=partly[:], op0=ALU.mult, op1=ALU.add
+    )
+
+    magnitude = pool.tile([P, SEQ_HALVES, PAIRS], F32, name="magnitude")
+    nc.vector.scalar_tensor_tensor(
+        out=magnitude[:], in0=reduced[:], scalar=-1.0, in1=reduced[:], op0=ALU.mult, op1=ALU.max
+    )
+    complement = pool.tile([P, SEQ_HALVES, PAIRS], F32, name="complement")
+    nc.vector.tensor_scalar(
+        out=complement[:], in0=magnitude[:], scalar1=-0.5, scalar2=math.pi / 2.0, op0=ALU.mult, op1=ALU.add
+    )
+    sin_half = pool.tile([P, SEQ_HALVES, PAIRS], F32, name="sin_half")
+    nc.scalar.activation(out=sin_half[:], in_=reduced[:], func=ACT.Sin, scale=0.5)
+    cos_half = pool.tile([P, SEQ_HALVES, PAIRS], F32, name="cos_half")
+    nc.scalar.activation(out=cos_half[:], in_=complement[:], func=ACT.Sin)
+
+    sine = pool.tile([P, SEQ_HALVES, PAIRS], F32, name="sine")
+    nc.vector.scalar_tensor_tensor(
+        out=sine[:], in0=sin_half[:], scalar=2.0, in1=cos_half[:], op0=ALU.mult, op1=ALU.mult
+    )
+    cos_less_one = pool.tile([P, SEQ_HALVES, PAIRS], F32, name="cos_less_one")
+    nc.vector.scalar_tensor_tensor(
+        out=cos_less_one[:], in0=sin_half[:], scalar=-2.0, in1=sin_half[:], op0=ALU.mult, op1=ALU.mult
+    )
+    cosine = pool.tile([P, SEQ_HALVES, PAIRS], F32, name="cosine")
+    nc.vector.tensor_scalar_add(out=cosine[:], in0=cos_less_one[:], scalar1=1.0)
+    mixed = pool.tile([P, SEQ_HALVES, PAIRS, 2], F32, name="mixed")
+    nc.vector.scalar_tensor_tensor(
+        out=mixed[:, :, :, 0], in0=cosine[:], scalar=-1.0, in1=sine[:], op0=ALU.mult, op1=ALU.subtract
+    )
+    nc.vector.scalar_tensor_tensor(
+        out=mixed[:, :, :, 1], in0=cosine[:], scalar=-1.0, in1=sine[:], op0=ALU.mult, op1=ALU.add
+    )
+    return cosine, mixed
+
+
+def tile_multilatentattention_pa_kernel(tc, x, Wqa, Wqb, out):
+    nc = tc.nc
+    x_rows = x.rearrange("b s d -> (b s) d")
+    out_rows = out.rearrange("b s h f -> (b s) (h f)")
+    wqb_by_partition = Wqb.rearrange("(p t) n -> p t n", t=PACK, p=P)
+
+    with ExitStack() as ctx:
+        keep = ctx.enter_context(tc.tile_pool(name="keep", bufs=1))
+        stage = ctx.enter_context(tc.tile_pool(name="stage", bufs=3))
+        results = ctx.enter_context(tc.tile_pool(name="results", bufs=6))
+        psum = ctx.enter_context(tc.psum_pool(name="psum", bufs=PSUM_BANKS))
+        ctx.enter_context(tc.manual_schedule())
+
+        a_raw = keep.tile([P, D_PASSES, PACK, Q_RANK], BF16, name="a_raw")
+        x_raw = keep.tile([P, TOKEN_TILES, D_MODEL], BF16, name="x_raw")
+        b_raw = keep.tile([P, CHUNKS, PACK, CHUNK_COLS], BF16, name="b_raw")
+
+        a_codes = keep.tile([P, D_PASSES, Q_RANK], U32, name="a_codes", align_bytes=64)
+        a_scales = keep.tile([P, D_PASSES, Q_RANK], U8, name="a_scales", align_bytes=64)
+        x_codes = keep.tile([P, TOKEN_TILES, D_PASSES, P], U32, name="x_codes", align_bytes=64)
+        x_scales = keep.tile([P, TOKEN_TILES, D_PASSES, P], U8, name="x_scales", align_bytes=64)
+        cq_codes = keep.tile([P, TOKEN_TILES, P], U32, name="cq_codes", align_bytes=64)
+        cq_scales = keep.tile([P, TOKEN_TILES, P], U8, name="cq_scales", align_bytes=64)
+        b_codes = keep.tile([P, CHUNKS, KINDS, BANK], U32, name="b_codes", align_bytes=64)
+        b_scales = keep.tile([P, CHUNKS, KINDS, BANK], U8, name="b_scales", align_bytes=64)
+
+        def load_b(chunk):
+            cols = slice(chunk * CHUNK_COLS, (chunk + 1) * CHUNK_COLS)
+            nc.sync.dma_start(out=b_raw[:, chunk], in_=wqb_by_partition[:, :, cols])
+
+        def load_a(g):
+            rows = Wqa[g * K_PASS : (g + 1) * K_PASS, :]
+            nc.sync.dma_start(
+                out=a_raw[:, g].rearrange("p t n -> p (t n)"),
+                in_=rows.rearrange("(p t) n -> p (t n)", p=P, t=PACK),
+            )
+
+        def load_x(i):
+            nc.sync.dma_start(out=x_raw[:, i, :], in_=x_rows[i * P : (i + 1) * P, :])
+
+        tiles_per_chunk = TOKEN_TILES // CHUNKS
+        load_b(0)
+        for g in range(D_PASSES):
+            load_a(g)
+        for i in range(TOKEN_TILES):
+            if i > 0 and i % tiles_per_chunk == 0:
+                load_b(i // tiles_per_chunk)
+            load_x(i)
+
+        identity = keep.tile([P, P], F32, name="identity")
+        make_identity(nc, identity[:])
+        cosine, mixed = build_rotation_tables(nc, keep)
+
+        b_grouped = {}
+
+        def regroup_b(copy, chunk, kind, first_head, heads):
+            if first_head == 0:
+                b_grouped[(chunk, kind)] = stage.tile(
+                    [P, BANK, PACK], BF16, name="b_grouped", tag="b_grouped", align_bytes=64
+                )
+            some = slice(first_head, first_head + heads)
+            grouped = b_grouped[(chunk, kind)]
+            if kind == PLAIN_KIND:
+                copy(
+                    out=grouped[:].rearrange("p (h c i) t -> p h c t i", h=CHUNK_HEADS, i=4)[:, some],
+                    in_=b_raw[:, chunk].rearrange(
+                        "p t (h k c i) -> p k h c t i", h=CHUNK_HEADS, k=KINDS, i=4
+                    )[:, PLAIN_KIND, some],
+                )
+            else:
+                for block in range(2):
+                    copy(
+                        out=grouped[:].rearrange(
+                            "p (b h c i) t -> p b h c t i", b=2, h=CHUNK_HEADS, i=4
+                        )[:, block, some],
+                        in_=b_raw[:, chunk].rearrange(
+                            "p t (h k c i e) -> p k e h c t i", h=CHUNK_HEADS, k=KINDS, i=4, e=2
+                        )[:, ROTARY_KIND, 1 - block, some],
+                    )
+
+        def quantise_b(chunk, kind):
+            nc.vector.quantize_mx(
+                out=b_codes[:, chunk, kind, :].bitcast(FP8X4),
+                scales=b_scales[:, chunk, kind, :],
+                in_=b_grouped[(chunk, kind)][:].rearrange("p n t -> p (n t)"),
+            )
+
+        def prepare_b(chunk, part):
+            if 1 <= chunk <= VECTOR_CHUNKS:
+                if part < KINDS:
+                    regroup_b(nc.vector.tensor_copy, chunk, KINDS - 1 - part, 0, CHUNK_HEADS)
+                else:
+                    quantise_b(chunk, 2 * KINDS - 1 - part)
+            else:
+                for kind in (ROTARY_KIND, PLAIN_KIND):
+                    regroup_b(nc.scalar.copy, chunk, kind, part, 1)
+                if part == CHUNK_HEADS - 1:
+                    for kind in (ROTARY_KIND, PLAIN_KIND):
+                        quantise_b(chunk, kind)
+
+        a_grouped = {}
+
+        def regroup_a(g):
+            a_grouped[g] = stage.tile([P, Q_RANK, PACK], BF16, name="a_grouped", tag="a_grouped", align_bytes=64)
+            nc.vector.tensor_copy(
+                out=a_grouped[g][:].rearrange("p (s m) t -> p s m t", s=RANK_TILES),
+                in_=a_raw[:, g].rearrange("p t (m s) -> p s m t", s=RANK_TILES),
+            )
+
+        def quantise_a(g):
+            nc.vector.quantize_mx(
+                out=a_codes[:, g, :].bitcast(FP8X4),
+                scales=a_scales[:, g, :],
+                in_=a_grouped[g][:].rearrange("p n t -> p (n t)"),
+            )
+
+        def quantise_x(i):
+            x_words = x_raw[:, i, :].bitcast(F32)
+            x_grouped = stage.tile([P, D_PASSES * P * PACK], BF16, name="x_grouped", align_bytes=64)
+            grouped_words = x_grouped[:].bitcast(F32).rearrange("p (g r u) -> p g r u", g=D_PASSES, r=P, u=2)
+            passes_per_bank = 2
+            for first_pass in range(0, D_PASSES, passes_per_bank):
+                turned = psum.tile([P, passes_per_bank * 2, P], F32, name="turned", tag="bank")
+                for c in range(passes_per_bank * 2):
+                    first_word = (first_pass + c // 2) * 2 * P + c % 2
+                    nc.tensor.transpose(
+                        turned[:, c, :], x_words[:, first_word : first_word - c % 2 + 2 * P : 2], identity[:]
+                    )
+                nc.scalar.copy(
+                    out=grouped_words[:, first_pass : first_pass + passes_per_bank],
+                    in_=turned[:].rearrange("p (g u) r -> p g r u", u=2),
+                )
+            nc.vector.quantize_mx(
+                out=x_codes[:, i].rearrange("p g r -> p (g r)").bitcast(FP8X4),
+                scales=x_scales[:, i].rearrange("p g r -> p (g r)"),
+                in_=x_grouped[:],
+            )
+
+        def first_product(i):
+            cq_bank = psum.tile([P, RANK_TILES, P], F32, name="cq_bank", tag="bank")
+            for t in range(RANK_TILES):
+                for g in range(D_PASSES):
+                    nc.tensor.matmul_mx(
+                        out=cq_bank[:, t, :],
+                        lhsT=a_codes[:, g, t * P : (t + 1) * P].bitcast(FP8X4),
+                        lhsT_scale=a_scales[:, g, t * P : (t + 1) * P],
+                        rhs=x_codes[:, i, g, :].bitcast(FP8X4),
+                        rhs_scale=x_scales[:, i, g, :],
+                        start=(g == 0),
+                        stop=(g == D_PASSES - 1),
+                    )
+            cq_grouped = stage.tile([P, P, PACK], BF16, name="cq_grouped", align_bytes=64)
+            nc.scalar.copy(out=cq_grouped[:], in_=cq_bank[:].rearrange("p t r -> p r t"))
+            nc.vector.quantize_mx(
+                out=cq_codes[:, i, :].bitcast(FP8X4),
+                scales=cq_scales[:, i, :],
+                in_=cq_grouped[:].rearrange("p r t -> p (r t)"),
+            )
+
+        def second_pass(i, bank, chunk, kind, cols, start, stop):
+            nc.tensor.matmul_mx(
+                out=bank,
+                lhsT=cq_codes[:, i, :].bitcast(FP8X4),
+                lhsT_scale=cq_scales[:, i, :],
+                rhs=b_codes[:, chunk, kind, cols].bitcast(FP8X4),
+                rhs_scale=b_scales[:, chunk, kind, cols],
+                start=start,
+                stop=stop,
+            )
+
+        unfinished = []
+
+        def second_product(i, chunk):
+            w_then_u = psum.tile([P, 2, CHUNK_PAIRS], F32, name="w_then_u", tag="bank")
+            second_pass(i, w_then_u[:].rearrange("p b n -> p (b n)"), chunk, ROTARY_KIND, slice(0, BANK), True, True)
+            u_plus_w = psum.tile([P, CHUNK_PAIRS], F32, name="u_plus_w", tag="bank")
+            second_pass(i, u_plus_w[:], chunk, ROTARY_KIND, slice(0, CHUNK_PAIRS), True, False)
+            second_pass(i, u_plus_w[:], chunk, ROTARY_KIND, slice(CHUNK_PAIRS, BANK), False, True)
+            plain = psum.tile([P, BANK], F32, name="plain", tag="bank")
+            second_pass(i, plain[:], chunk, PLAIN_KIND, slice(0, BANK), True, True)
+
+            half = i % SEQ_HALVES
+            heads = results.tile([P, CHUNK_HEADS, HEAD], F32, name="heads")
+            nc.vector.tensor_tensor(
+                out=heads[:, :, PLAIN:HEAD].rearrange("p h (j e) -> p h j e", e=2),
+                in0=w_then_u[:].rearrange("p b (h j) -> p h j b", h=CHUNK_HEADS),
+                in1=mixed[:, half].unsqueeze(1).to_broadcast([P, CHUNK_HEADS, PAIRS, 2]),
+                op=ALU.mult,
+            )
+            shared = results.tile([P, CHUNK_HEADS, PAIRS], F32, name="shared")
+            nc.vector.tensor_tensor(
+                out=shared[:],
+                in0=u_plus_w[:].rearrange("p (h j) -> p h j", h=CHUNK_HEADS),
+                in1=cosine[:, half].unsqueeze(1).to_broadcast([P, CHUNK_HEADS, PAIRS]),
+                op=ALU.mult,
+            )
+            nc.scalar.copy(
+                out=heads[:, :, 0:PLAIN], in_=plain[:].rearrange("p (h f) -> p h f", h=CHUNK_HEADS)
+            )
+            if unfinished:
+                add_and_store(*unfinished[-1])
+            unfinished.append((i, chunk, heads, shared))
+
+        def add_and_store(i, chunk, heads, shared):
+            adder = nc.vector if i % VECTOR_ADDS == VECTOR_ADDS - 1 else nc.gpsimd
+            rotated = heads[:, :, PLAIN:HEAD].rearrange("p h (j e) -> p h j e", e=2)
+            adder.tensor_tensor(
+                out=rotated,
+                in0=rotated,
+                in1=shared[:].unsqueeze(3).to_broadcast([P, CHUNK_HEADS, PAIRS, 2]),
+                op=ALU.add,
+            )
+            nc.sync.dma_start(
+                out=out_rows[i * P : (i + 1) * P, chunk * CHUNK_COLS : (chunk + 1) * CHUNK_COLS],
+                in_=heads[:].rearrange("p h f -> p (h f)"),
+            )
+
+        for g in range(D_PASSES + 1):
+            if g < D_PASSES:
+                regroup_a(g)
+            if g > 0:
+                quantise_a(g - 1)
+        for part in range(PREPARE_STEPS):
+            prepare_b(0, part)
+
+        assert PREPARE_STEPS * (CHUNKS - 1) <= LAG + 1 + CHUNK_LAG * (CHUNKS - 1)
+        for step in range(TOKEN_TILES + LAG + 1 + CHUNK_LAG * (CHUNKS - 1)):
+            if step < TOKEN_TILES:
+                quantise_x(step)
+            if LAG <= step < TOKEN_TILES + LAG:
+                first_product(step - LAG)
+            if step < PREPARE_STEPS * (CHUNKS - 1):
+                prepare_b(1 + step // PREPARE_STEPS, step % PREPARE_STEPS)
+            for chunk in range(CHUNKS):
+                i = step - LAG - 1 - CHUNK_LAG * chunk
+                if 0 <= i < TOKEN_TILES:
+                    second_product(i, chunk)
+        add_and_store(*unfinished[-1])

@@ -39,10 +39,11 @@ CHUNK_PAIRS = CHUNK_HEADS * PAIRS
 KINDS = 2
 PLAIN_KIND, ROTARY_KIND = 0, 1
 
-LAG = 2
+TURN_AHEAD = 2
 CHUNK_LAG = 3
 PREPARE_STEPS = 4
 VECTOR_CHUNKS = 2
+SCALAR_PASS = 2
 VECTOR_ADDS = 4
 PSUM_BANKS = 8
 
@@ -54,7 +55,7 @@ TWO_PI_LOW = TWO_PI - TWO_PI_HIGH
 ROUND_MAGIC = 1.5 * 2.0**23
 
 
-def build_rotation_tables(nc, pool):
+def build_half_angle_sines(nc, pool):
     position_int = pool.tile([P, SEQ_HALVES], I32, name="position_int")
     nc.gpsimd.iota(position_int[:], pattern=[[P, SEQ_HALVES]], base=0, channel_multiplier=1)
     position = pool.tile([P, SEQ_HALVES], F32, name="position")
@@ -101,7 +102,10 @@ def build_rotation_tables(nc, pool):
     nc.scalar.activation(out=sin_half[:], in_=reduced[:], func=ACT.Sin, scale=0.5)
     cos_half = pool.tile([P, SEQ_HALVES, PAIRS], F32, name="cos_half")
     nc.scalar.activation(out=cos_half[:], in_=complement[:], func=ACT.Sin)
+    return sin_half, cos_half
 
+
+def build_rotation_tables(nc, pool, sin_half, cos_half):
     sine = pool.tile([P, SEQ_HALVES, PAIRS], F32, name="sine")
     nc.vector.scalar_tensor_tensor(
         out=sine[:], in0=sin_half[:], scalar=2.0, in1=cos_half[:], op0=ALU.mult, op1=ALU.mult
@@ -131,7 +135,7 @@ def tile_multilatentattention_pa_kernel(tc, x, Wqa, Wqb, out):
     with ExitStack() as ctx:
         keep = ctx.enter_context(tc.tile_pool(name="keep", bufs=1))
         stage = ctx.enter_context(tc.tile_pool(name="stage", bufs=3))
-        results = ctx.enter_context(tc.tile_pool(name="results", bufs=6))
+        results = ctx.enter_context(tc.tile_pool(name="results", bufs=11))
         psum = ctx.enter_context(tc.psum_pool(name="psum", bufs=PSUM_BANKS))
         ctx.enter_context(tc.manual_schedule())
 
@@ -163,17 +167,17 @@ def tile_multilatentattention_pa_kernel(tc, x, Wqa, Wqb, out):
             nc.sync.dma_start(out=x_raw[:, i, :], in_=x_rows[i * P : (i + 1) * P, :])
 
         tiles_per_chunk = TOKEN_TILES // CHUNKS
-        load_b(0)
-        for g in range(D_PASSES):
-            load_a(g)
         for i in range(TOKEN_TILES):
-            if i > 0 and i % tiles_per_chunk == 0:
-                load_b(i // tiles_per_chunk)
             load_x(i)
+            if i == 0:
+                for g in range(D_PASSES):
+                    load_a(g)
+            if i % tiles_per_chunk == tiles_per_chunk - 1:
+                load_b(i // tiles_per_chunk)
 
+        sin_half, cos_half = build_half_angle_sines(nc, keep)
         identity = keep.tile([P, P], F32, name="identity")
         make_identity(nc, identity[:])
-        cosine, mixed = build_rotation_tables(nc, keep)
 
         b_grouped = {}
 
@@ -210,7 +214,7 @@ def tile_multilatentattention_pa_kernel(tc, x, Wqa, Wqb, out):
             )
 
         def prepare_b(chunk, part):
-            if 1 <= chunk <= VECTOR_CHUNKS:
+            if chunk < VECTOR_CHUNKS:
                 if part < KINDS:
                     regroup_b(nc.vector.tensor_copy, chunk, KINDS - 1 - part, 0, CHUNK_HEADS)
                 else:
@@ -226,7 +230,8 @@ def tile_multilatentattention_pa_kernel(tc, x, Wqa, Wqb, out):
 
         def regroup_a(g):
             a_grouped[g] = stage.tile([P, Q_RANK, PACK], BF16, name="a_grouped", tag="a_grouped", align_bytes=64)
-            nc.vector.tensor_copy(
+            copy = nc.scalar.copy if g == SCALAR_PASS else nc.vector.tensor_copy
+            copy(
                 out=a_grouped[g][:].rearrange("p (s m) t -> p s m t", s=RANK_TILES),
                 in_=a_raw[:, g].rearrange("p t (m s) -> p s m t", s=RANK_TILES),
             )
@@ -238,10 +243,14 @@ def tile_multilatentattention_pa_kernel(tc, x, Wqa, Wqb, out):
                 in_=a_grouped[g][:].rearrange("p n t -> p (n t)"),
             )
 
-        def quantise_x(i):
+        x_grouped = {}
+
+        def turn_x(i):
             x_words = x_raw[:, i, :].bitcast(F32)
-            x_grouped = stage.tile([P, D_PASSES * P * PACK], BF16, name="x_grouped", align_bytes=64)
-            grouped_words = x_grouped[:].bitcast(F32).rearrange("p (g r u) -> p g r u", g=D_PASSES, r=P, u=2)
+            x_grouped[i] = stage.tile(
+                [P, D_PASSES * P * PACK], BF16, name="x_grouped", tag="x_grouped", align_bytes=64
+            )
+            grouped_words = x_grouped[i][:].bitcast(F32).rearrange("p (g r u) -> p g r u", g=D_PASSES, r=P, u=2)
             passes_per_bank = 2
             for first_pass in range(0, D_PASSES, passes_per_bank):
                 turned = psum.tile([P, passes_per_bank * 2, P], F32, name="turned", tag="bank")
@@ -254,11 +263,15 @@ def tile_multilatentattention_pa_kernel(tc, x, Wqa, Wqb, out):
                     out=grouped_words[:, first_pass : first_pass + passes_per_bank],
                     in_=turned[:].rearrange("p (g u) r -> p g r u", u=2),
                 )
+
+        def quantise_x(i):
             nc.vector.quantize_mx(
                 out=x_codes[:, i].rearrange("p g r -> p (g r)").bitcast(FP8X4),
                 scales=x_scales[:, i].rearrange("p g r -> p (g r)"),
-                in_=x_grouped[:],
+                in_=x_grouped[i][:],
             )
+
+        cq_grouped = {}
 
         def first_product(i):
             cq_bank = psum.tile([P, RANK_TILES, P], F32, name="cq_bank", tag="bank")
@@ -273,12 +286,14 @@ def tile_multilatentattention_pa_kernel(tc, x, Wqa, Wqb, out):
                         start=(g == 0),
                         stop=(g == D_PASSES - 1),
                     )
-            cq_grouped = stage.tile([P, P, PACK], BF16, name="cq_grouped", align_bytes=64)
-            nc.scalar.copy(out=cq_grouped[:], in_=cq_bank[:].rearrange("p t r -> p r t"))
+            cq_grouped[i] = stage.tile([P, P, PACK], BF16, name="cq_grouped", tag="cq_grouped", align_bytes=64)
+            nc.scalar.copy(out=cq_grouped[i][:], in_=cq_bank[:].rearrange("p t r -> p r t"))
+
+        def quantise_cq(i):
             nc.vector.quantize_mx(
                 out=cq_codes[:, i, :].bitcast(FP8X4),
                 scales=cq_scales[:, i, :],
-                in_=cq_grouped[:].rearrange("p r t -> p (r t)"),
+                in_=cq_grouped[i][:].rearrange("p r t -> p (r t)"),
             )
 
         def second_pass(i, bank, chunk, kind, cols, start, stop):
@@ -339,24 +354,39 @@ def tile_multilatentattention_pa_kernel(tc, x, Wqa, Wqb, out):
                 in_=heads[:].rearrange("p h f -> p (h f)"),
             )
 
-        for g in range(D_PASSES + 1):
-            if g < D_PASSES:
-                regroup_a(g)
-            if g > 0:
+        turn_x(0)
+        for g in range(D_PASSES):
+            regroup_a(g)
+            if g == 0:
+                quantise_x(0)
+            else:
                 quantise_a(g - 1)
-        for part in range(PREPARE_STEPS):
-            prepare_b(0, part)
+        turn_x(1)
+        cosine, mixed = build_rotation_tables(nc, keep, sin_half, cos_half)
+        regroup_b(nc.vector.tensor_copy, 0, ROTARY_KIND, 0, CHUNK_HEADS)
+        quantise_a(D_PASSES - 1)
+        quantise_x(1)
+        regroup_b(nc.vector.tensor_copy, 0, PLAIN_KIND, 0, CHUNK_HEADS)
+        quantise_b(0, ROTARY_KIND)
 
-        assert PREPARE_STEPS * (CHUNKS - 1) <= LAG + 1 + CHUNK_LAG * (CHUNKS - 1)
-        for step in range(TOKEN_TILES + LAG + 1 + CHUNK_LAG * (CHUNKS - 1)):
+        assert PREPARE_STEPS <= CHUNK_LAG + 1
+        for step in range(TOKEN_TILES + 1 + CHUNK_LAG * (CHUNKS - 1)):
+            if step + TURN_AHEAD < TOKEN_TILES:
+                turn_x(step + TURN_AHEAD)
             if step < TOKEN_TILES:
-                quantise_x(step)
-            if LAG <= step < TOKEN_TILES + LAG:
-                first_product(step - LAG)
-            if step < PREPARE_STEPS * (CHUNKS - 1):
-                prepare_b(1 + step // PREPARE_STEPS, step % PREPARE_STEPS)
+                first_product(step)
+            if step == 0:
+                quantise_b(0, PLAIN_KIND)
             for chunk in range(CHUNKS):
-                i = step - LAG - 1 - CHUNK_LAG * chunk
+                i = step - 1 - CHUNK_LAG * chunk
                 if 0 <= i < TOKEN_TILES:
                     second_product(i, chunk)
+            if step < TOKEN_TILES:
+                quantise_cq(step)
+            for chunk in range(1, CHUNKS):
+                part = step - CHUNK_LAG * (chunk - 1)
+                if 0 <= part < PREPARE_STEPS:
+                    prepare_b(chunk, part)
+            if step + TURN_AHEAD < TOKEN_TILES:
+                quantise_x(step + TURN_AHEAD)
         add_and_store(*unfinished[-1])

@@ -40,11 +40,16 @@ KINDS = 2
 PLAIN_KIND, ROTARY_KIND = 0, 1
 
 TURN_AHEAD = 2
-CHUNK_LAG = 3
+PIECES_RAMP = (2, 2)
+PIECES = 3
+LAST_HEADS = 2
+RAMP = (0, 1, 1, 2)
+FULL_RATE = 3
+CHUNK_LAG = 2
 PREPARE_STEPS = 4
-VECTOR_CHUNKS = 2
-SCALAR_PASS = 2
-VECTOR_ADDS = 4
+SCALAR_KINDS = ((2, PLAIN_KIND), (3, ROTARY_KIND), (3, PLAIN_KIND))
+SCALAR_PASSES = (1, 3)
+VECTOR_ADDS = 3
 PSUM_BANKS = 8
 
 FLOPS = 2 * TOKENS * D_MODEL * Q_RANK + 2 * TOKENS * Q_RANK * HEADS * HEAD
@@ -135,12 +140,13 @@ def tile_multilatentattention_pa_kernel(tc, x, Wqa, Wqb, out):
     with ExitStack() as ctx:
         keep = ctx.enter_context(tc.tile_pool(name="keep", bufs=1))
         stage = ctx.enter_context(tc.tile_pool(name="stage", bufs=3))
+        arrivals = ctx.enter_context(tc.tile_pool(name="arrivals", bufs=6))
         results = ctx.enter_context(tc.tile_pool(name="results", bufs=11))
         psum = ctx.enter_context(tc.psum_pool(name="psum", bufs=PSUM_BANKS))
         ctx.enter_context(tc.manual_schedule())
 
         a_raw = keep.tile([P, D_PASSES, PACK, Q_RANK], BF16, name="a_raw")
-        x_raw = keep.tile([P, TOKEN_TILES, D_MODEL], BF16, name="x_raw")
+        x_raw = {}
         b_raw = keep.tile([P, CHUNKS, PACK, CHUNK_COLS], BF16, name="b_raw")
 
         a_codes = keep.tile([P, D_PASSES, Q_RANK], U32, name="a_codes", align_bytes=64)
@@ -164,7 +170,8 @@ def tile_multilatentattention_pa_kernel(tc, x, Wqa, Wqb, out):
             )
 
         def load_x(i):
-            nc.sync.dma_start(out=x_raw[:, i, :], in_=x_rows[i * P : (i + 1) * P, :])
+            x_raw[i] = arrivals.tile([P, D_MODEL], BF16, name="x_raw", tag="x_raw")
+            nc.sync.dma_start(out=x_raw[i][:], in_=x_rows[i * P : (i + 1) * P, :])
 
         tiles_per_chunk = TOKEN_TILES // CHUNKS
         for i in range(TOKEN_TILES):
@@ -206,31 +213,34 @@ def tile_multilatentattention_pa_kernel(tc, x, Wqa, Wqb, out):
                         )[:, ROTARY_KIND, 1 - block, some],
                     )
 
+        quantised_chunks = set()
+
         def quantise_b(chunk, kind):
+            if kind == PLAIN_KIND:
+                quantised_chunks.add(chunk)
             nc.vector.quantize_mx(
                 out=b_codes[:, chunk, kind, :].bitcast(FP8X4),
                 scales=b_scales[:, chunk, kind, :],
                 in_=b_grouped[(chunk, kind)][:].rearrange("p n t -> p (n t)"),
             )
 
-        def prepare_b(chunk, part):
-            if chunk < VECTOR_CHUNKS:
-                if part < KINDS:
-                    regroup_b(nc.vector.tensor_copy, chunk, KINDS - 1 - part, 0, CHUNK_HEADS)
+        def prepare_b(chunk):
+            pieces = []
+            for kind in (ROTARY_KIND, PLAIN_KIND):
+                if (chunk, kind) in SCALAR_KINDS:
+                    for head in range(CHUNK_HEADS):
+                        pieces.append(lambda kind=kind, head=head: regroup_b(nc.scalar.copy, chunk, kind, head, 1))
                 else:
-                    quantise_b(chunk, 2 * KINDS - 1 - part)
-            else:
-                for kind in (ROTARY_KIND, PLAIN_KIND):
-                    regroup_b(nc.scalar.copy, chunk, kind, part, 1)
-                if part == CHUNK_HEADS - 1:
-                    for kind in (ROTARY_KIND, PLAIN_KIND):
-                        quantise_b(chunk, kind)
+                    pieces.append(lambda kind=kind: regroup_b(nc.vector.tensor_copy, chunk, kind, 0, CHUNK_HEADS))
+            for kind in (ROTARY_KIND, PLAIN_KIND):
+                pieces.append(lambda kind=kind: quantise_b(chunk, kind))
+            return pieces
 
         a_grouped = {}
 
         def regroup_a(g):
-            a_grouped[g] = stage.tile([P, Q_RANK, PACK], BF16, name="a_grouped", tag="a_grouped", align_bytes=64)
-            copy = nc.scalar.copy if g == SCALAR_PASS else nc.vector.tensor_copy
+            a_grouped[g] = stage.tile([P, Q_RANK, PACK], BF16, name="a_grouped", tag="a_grouped", bufs=D_PASSES, align_bytes=64)
+            copy = nc.scalar.copy if g in SCALAR_PASSES else nc.vector.tensor_copy
             copy(
                 out=a_grouped[g][:].rearrange("p (s m) t -> p s m t", s=RANK_TILES),
                 in_=a_raw[:, g].rearrange("p t (m s) -> p s m t", s=RANK_TILES),
@@ -246,7 +256,7 @@ def tile_multilatentattention_pa_kernel(tc, x, Wqa, Wqb, out):
         x_grouped = {}
 
         def turn_x(i):
-            x_words = x_raw[:, i, :].bitcast(F32)
+            x_words = x_raw[i][:].bitcast(F32)
             x_grouped[i] = stage.tile(
                 [P, D_PASSES * P * PACK], BF16, name="x_grouped", tag="x_grouped", align_bytes=64
             )
@@ -341,52 +351,60 @@ def tile_multilatentattention_pa_kernel(tc, x, Wqa, Wqb, out):
             unfinished.append((i, chunk, heads, shared))
 
         def add_and_store(i, chunk, heads, shared):
-            adder = nc.vector if i % VECTOR_ADDS == VECTOR_ADDS - 1 else nc.gpsimd
-            rotated = heads[:, :, PLAIN:HEAD].rearrange("p h (j e) -> p h j e", e=2)
-            adder.tensor_tensor(
-                out=rotated,
-                in0=rotated,
-                in1=shared[:].unsqueeze(3).to_broadcast([P, CHUNK_HEADS, PAIRS, 2]),
-                op=ALU.add,
-            )
-            nc.sync.dma_start(
-                out=out_rows[i * P : (i + 1) * P, chunk * CHUNK_COLS : (chunk + 1) * CHUNK_COLS],
-                in_=heads[:].rearrange("p h f -> p (h f)"),
-            )
+            left = TOKEN_TILES * CHUNKS - len(unfinished)
+            adder = nc.gpsimd if len(unfinished) % VECTOR_ADDS > 0 and left > 1 else nc.vector
+            share = CHUNK_HEADS if left else LAST_HEADS
+            for first in range(0, CHUNK_HEADS, share):
+                some = slice(first, first + share)
+                rotated = heads[:, some, PLAIN:HEAD].rearrange("p h (j e) -> p h j e", e=2)
+                adder.tensor_tensor(
+                    out=rotated,
+                    in0=rotated,
+                    in1=shared[:, some].unsqueeze(3).to_broadcast([P, share, PAIRS, 2]),
+                    op=ALU.add,
+                )
+                first_col = chunk * CHUNK_COLS + first * HEAD
+                nc.sync.dma_start(
+                    out=out_rows[i * P : (i + 1) * P, first_col : first_col + share * HEAD],
+                    in_=heads[:, some].rearrange("p h f -> p (h f)"),
+                )
 
         turn_x(0)
         for g in range(D_PASSES):
             regroup_a(g)
             if g == 0:
                 quantise_x(0)
-            else:
-                quantise_a(g - 1)
         turn_x(1)
-        cosine, mixed = build_rotation_tables(nc, keep, sin_half, cos_half)
-        regroup_b(nc.vector.tensor_copy, 0, ROTARY_KIND, 0, CHUNK_HEADS)
-        quantise_a(D_PASSES - 1)
+        for g in range(D_PASSES):
+            quantise_a(g)
+            if g == 0:
+                cosine, mixed = build_rotation_tables(nc, keep, sin_half, cos_half)
         quantise_x(1)
+        regroup_b(nc.vector.tensor_copy, 0, ROTARY_KIND, 0, CHUNK_HEADS)
         regroup_b(nc.vector.tensor_copy, 0, PLAIN_KIND, 0, CHUNK_HEADS)
         quantise_b(0, ROTARY_KIND)
 
-        assert PREPARE_STEPS <= CHUNK_LAG + 1
-        for step in range(TOKEN_TILES + 1 + CHUNK_LAG * (CHUNKS - 1)):
+        units = sorted(((i, c) for i in range(TOKEN_TILES) for c in range(CHUNKS)), key=lambda u: (u[0] + CHUNK_LAG * u[1], u[1]))
+        pieces = [piece for chunk in range(1, CHUNKS) for piece in prepare_b(chunk)]
+        for step in range(TOKEN_TILES * CHUNKS // FULL_RATE + len(RAMP)):
             if step + TURN_AHEAD < TOKEN_TILES:
                 turn_x(step + TURN_AHEAD)
             if step < TOKEN_TILES:
                 first_product(step)
             if step == 0:
                 quantise_b(0, PLAIN_KIND)
-            for chunk in range(CHUNKS):
-                i = step - 1 - CHUNK_LAG * chunk
-                if 0 <= i < TOKEN_TILES:
+            for unused in range(RAMP[step] if step < len(RAMP) else FULL_RATE):
+                ready = [unit for unit in units if unit[0] < step and unit[1] in quantised_chunks]
+                if ready:
+                    i, chunk = ready[0]
+                    units.remove(ready[0])
                     second_product(i, chunk)
             if step < TOKEN_TILES:
                 quantise_cq(step)
-            for chunk in range(1, CHUNKS):
-                part = step - CHUNK_LAG * (chunk - 1)
-                if 0 <= part < PREPARE_STEPS:
-                    prepare_b(chunk, part)
+            for unused in range(PIECES_RAMP[step] if step < len(PIECES_RAMP) else PIECES):
+                if pieces:
+                    pieces.pop(0)()
             if step + TURN_AHEAD < TOKEN_TILES:
                 quantise_x(step + TURN_AHEAD)
+        assert not units and not pieces
         add_and_store(*unfinished[-1])

@@ -40,16 +40,16 @@ KINDS = 2
 PLAIN_KIND, ROTARY_KIND = 0, 1
 
 TURN_AHEAD = 2
-PIECES_RAMP = (2, 2)
+PIECES_RAMP = (1, 1, 2)
 PIECES = 3
 LAST_HEADS = 2
-RAMP = (0, 1, 1, 2)
-FULL_RATE = 3
-CHUNK_LAG = 2
+RAMP = (0, 1, 1, 1, 2)
+FULL_RATE = 4
+CHUNK_LAG = 1
 PREPARE_STEPS = 4
 SCALAR_KINDS = ((2, PLAIN_KIND), (3, ROTARY_KIND), (3, PLAIN_KIND))
-SCALAR_PASSES = (1, 3)
-VECTOR_ADDS = 3
+SCALAR_PASSES = (2,)
+VECTOR_ADDS = 4
 PSUM_BANKS = 8
 
 FLOPS = 2 * TOKENS * D_MODEL * Q_RANK + 2 * TOKENS * Q_RANK * HEADS * HEAD
@@ -386,7 +386,7 @@ def tile_multilatentattention_pa_kernel(tc, x, Wqa, Wqb, out):
 
         units = sorted(((i, c) for i in range(TOKEN_TILES) for c in range(CHUNKS)), key=lambda u: (u[0] + CHUNK_LAG * u[1], u[1]))
         pieces = [piece for chunk in range(1, CHUNKS) for piece in prepare_b(chunk)]
-        for step in range(TOKEN_TILES * CHUNKS // FULL_RATE + len(RAMP)):
+        for step in range(TOKEN_TILES * CHUNKS // FULL_RATE + 2 * len(RAMP)):
             if step + TURN_AHEAD < TOKEN_TILES:
                 turn_x(step + TURN_AHEAD)
             if step < TOKEN_TILES:

@@ -240,11 +240,13 @@ def tile_multilatentattention_pa_kernel(tc, x, Wqa, Wqb, out):
 
         def regroup_a(g):
             a_grouped[g] = stage.tile([P, Q_RANK, PACK], BF16, name="a_grouped", tag="a_grouped", bufs=D_PASSES, align_bytes=64)
-            copy = nc.scalar.copy if g in SCALAR_PASSES else nc.vector.tensor_copy
-            copy(
-                out=a_grouped[g][:].rearrange("p (s m) t -> p s m t", s=RANK_TILES),
-                in_=a_raw[:, g].rearrange("p t (m s) -> p s m t", s=RANK_TILES),
-            )
+            grouped = a_grouped[g][:].rearrange("p (s c i) t -> p s c t i", s=RANK_TILES, i=4)
+            raw = a_raw[:, g].rearrange("p t (c i s) -> p s c t i", s=RANK_TILES, i=4)
+            if g in SCALAR_PASSES:
+                for s in range(RANK_TILES):
+                    nc.scalar.copy(out=grouped[:, s], in_=raw[:, s])
+            else:
+                nc.vector.tensor_copy(out=grouped, in_=raw)
 
         def quantise_a(g):
             nc.vector.quantize_mx(
@@ -381,7 +383,8 @@ def tile_multilatentattention_pa_kernel(tc, x, Wqa, Wqb, out):
                 cosine, mixed = build_rotation_tables(nc, keep, sin_half, cos_half)
         quantise_x(1)
         regroup_b(nc.vector.tensor_copy, 0, ROTARY_KIND, 0, CHUNK_HEADS)
-        regroup_b(nc.vector.tensor_copy, 0, PLAIN_KIND, 0, CHUNK_HEADS)
+        for head in range(CHUNK_HEADS):
+            regroup_b(nc.scalar.copy, 0, PLAIN_KIND, head, 1)
         quantise_b(0, ROTARY_KIND)
 
         units = sorted(((i, c) for i in range(TOKEN_TILES) for c in range(CHUNKS)), key=lambda u: (u[0] + CHUNK_LAG * u[1], u[1]))

import math
from contextlib import ExitStack

import concourse.mybir as mybir
from concourse.masks import make_identity

F32 = mybir.dt.float32
BF16 = mybir.dt.bfloat16
I32 = mybir.dt.int32
U32 = mybir.dt.uint32
U8 = mybir.dt.uint8
FP8X4 = mybir.dt.float8_e4m3fn_x4
ALU = mybir.AluOpType
ACT = mybir.ActivationFunctionType

P = 128
PACK = 4
K_PASS = P * PACK

BATCH, SEQ, D_MODEL, HEADS, Q_RANK = 4, 256, 2048, 16, 512
PLAIN, ROTARY = 128, 128
HEAD = PLAIN + ROTARY
PAIRS = ROTARY // 2
PAIR_BITS = 6
assert 2**PAIR_BITS == PAIRS
ROPE_BASE = 10000.0

TOKENS = BATCH * SEQ
TOKEN_TILES = TOKENS // P
SEQ_HALVES = SEQ // P
D_PASSES = D_MODEL // K_PASS
RANK_TILES = Q_RANK // P

CHUNK_HEADS = 4
CHUNKS = HEADS // CHUNK_HEADS
CHUNK_COLS = CHUNK_HEADS * HEAD
BANK = CHUNK_HEADS * PLAIN
CHUNK_PAIRS = CHUNK_HEADS * PAIRS
KINDS = 2
PLAIN_KIND, ROTARY_KIND = 0, 1

TURN_AHEAD = 2
PIECES_RAMP = (1, 1, 2)
PIECES = 3
LAST_HEADS = 2
RAMP = (0, 1, 1, 1, 2)
FULL_RATE = 4
CHUNK_LAG = 1
PREPARE_STEPS = 4
SCALAR_KINDS = ((2, PLAIN_KIND), (3, ROTARY_KIND), (3, PLAIN_KIND))
SCALAR_PASSES = (2,)
VECTOR_ADDS = 4
PSUM_BANKS = 8

FLOPS = 2 * TOKENS * D_MODEL * Q_RANK + 2 * TOKENS * Q_RANK * HEADS * HEAD

TWO_PI = 2.0 * math.pi
TWO_PI_HIGH = round(TWO_PI * 2.0**15) / 2.0**15
TWO_PI_LOW = TWO_PI - TWO_PI_HIGH
ROUND_MAGIC = 1.5 * 2.0**23


def build_half_angle_sines(nc, pool):
    position_int = pool.tile([P, SEQ_HALVES], I32, name="position_int")
    nc.gpsimd.iota(position_int[:], pattern=[[P, SEQ_HALVES]], base=0, channel_multiplier=1)
    position = pool.tile([P, SEQ_HALVES], F32, name="position")
    nc.vector.tensor_copy(out=position[:], in_=position_int[:])

    ratio = ROPE_BASE ** (-2.0 / ROTARY)
    frequency = pool.tile([P, PAIRS], F32, name="frequency")
    nc.vector.memset(frequency[:, 0:1], 1.0)
    for doubling in range(PAIR_BITS):
        filled = 2**doubling
        nc.vector.tensor_scalar_mul(
            out=frequency[:, filled : 2 * filled], in0=frequency[:, 0:filled], scalar1=ratio**filled
        )

    angle = pool.tile([P, SEQ_HALVES, PAIRS], F32, name="angle")
    for half in range(SEQ_HALVES):
        nc.vector.tensor_scalar_mul(
            out=angle[:, half, :], in0=frequency[:], scalar1=position[:, half : half + 1]
        )

    turns = pool.tile([P, SEQ_HALVES, PAIRS], F32, name="turns")
    nc.vector.tensor_scalar(
        out=turns[:], in0=angle[:], scalar1=1.0 / TWO_PI, scalar2=ROUND_MAGIC, op0=ALU.mult, op1=ALU.add
    )
    nc.vector.tensor_scalar_sub(out=turns[:], in0=turns[:], scalar1=ROUND_MAGIC)
    partly = pool.tile([P, SEQ_HALVES, PAIRS], F32, name="partly")
    nc.vector.scalar_tensor_tensor(
        out=partly[:], in0=turns[:], scalar=-TWO_PI_HIGH, in1=angle[:], op0=ALU.mult, op1=ALU.add
    )
    reduced = pool.tile([P, SEQ_HALVES, PAIRS], F32, name="reduced")
    nc.vector.scalar_tensor_tensor(
        out=reduced[:], in0=turns[:], scalar=-TWO_PI_LOW, in1=partly[:], op0=ALU.mult, op1=ALU.add
    )

    magnitude = pool.tile([P, SEQ_HALVES, PAIRS], F32, name="magnitude")
    nc.vector.scalar_tensor_tensor(
        out=magnitude[:], in0=reduced[:], scalar=-1.0, in1=reduced[:], op0=ALU.mult, op1=ALU.max
    )
    complement = pool.tile([P, SEQ_HALVES, PAIRS], F32, name="complement")
    nc.vector.tensor_scalar(
        out=complement[:], in0=magnitude[:], scalar1=-0.5, scalar2=math.pi / 2.0, op0=ALU.mult, op1=ALU.add
    )
    sin_half = pool.tile([P, SEQ_HALVES, PAIRS], F32, name="sin_half")
    nc.scalar.activation(out=sin_half[:], in_=reduced[:], func=ACT.Sin, scale=0.5)
    cos_half = pool.tile([P, SEQ_HALVES, PAIRS], F32, name="cos_half")
    nc.scalar.activation(out=cos_half[:], in_=complement[:], func=ACT.Sin)
    return sin_half, cos_half


def build_rotation_tables(nc, pool, sin_half, cos_half):
    sine = pool.tile([P, SEQ_HALVES, PAIRS], F32, name="sine")
    nc.vector.scalar_tensor_tensor(
        out=sine[:], in0=sin_half[:], scalar=2.0, in1=cos_half[:], op0=ALU.mult, op1=ALU.mult
    )
    cos_less_one = pool.tile([P, SEQ_HALVES, PAIRS], F32, name="cos_less_one")
    nc.vector.scalar_tensor_tensor(
        out=cos_less_one[:], in0=sin_half[:], scalar=-2.0, in1=sin_half[:], op0=ALU.mult, op1=ALU.mult
    )
    cosine = pool.tile([P, SEQ_HALVES, PAIRS], F32, name="cosine")
    nc.vector.tensor_scalar_add(out=cosine[:], in0=cos_less_one[:], scalar1=1.0)
    mixed = pool.tile([P, SEQ_HALVES, PAIRS, 2], F32, name="mixed")
    nc.vector.scalar_tensor_tensor(
        out=mixed[:, :, :, 0], in0=cosine[:], scalar=-1.0, in1=sine[:], op0=ALU.mult, op1=ALU.subtract
    )
    nc.vector.scalar_tensor_tensor(
        out=mixed[:, :, :, 1], in0=cosine[:], scalar=-1.0, in1=sine[:], op0=ALU.mult, op1=ALU.add
    )
    return cosine, mixed


def tile_multilatentattention_pa_kernel(tc, x, Wqa, Wqb, out):
    nc = tc.nc
    x_rows = x.rearrange("b s d -> (b s) d")
    out_rows = out.rearrange("b s h f -> (b s) (h f)")
    wqb_by_partition = Wqb.rearrange("(p t) n -> p t n", t=PACK, p=P)

    with ExitStack() as ctx:
        keep = ctx.enter_context(tc.tile_pool(name="keep", bufs=1))
        stage = ctx.enter_context(tc.tile_pool(name="stage", bufs=3))
        arrivals = ctx.enter_context(tc.tile_pool(name="arrivals", bufs=6))
        results = ctx.enter_context(tc.tile_pool(name="results", bufs=11))
        psum = ctx.enter_context(tc.psum_pool(name="psum", bufs=PSUM_BANKS))
        ctx.enter_context(tc.manual_schedule())

        a_raw = keep.tile([P, D_PASSES, PACK, Q_RANK], BF16, name="a_raw")
        x_raw = {}
        b_raw = keep.tile([P, CHUNKS, PACK, CHUNK_COLS], BF16, name="b_raw")

        a_codes = keep.tile([P, D_PASSES, Q_RANK], U32, name="a_codes", align_bytes=64)
        a_scales = keep.tile([P, D_PASSES, Q_RANK], U8, name="a_scales", align_bytes=64)
        x_codes = keep.tile([P, TOKEN_TILES, D_PASSES, P], U32, name="x_codes", align_bytes=64)
        x_scales = keep.tile([P, TOKEN_TILES, D_PASSES, P], U8, name="x_scales", align_bytes=64)
        cq_codes = keep.tile([P, TOKEN_TILES, P], U32, name="cq_codes", align_bytes=64)
        cq_scales = keep.tile([P, TOKEN_TILES, P], U8, name="cq_scales", align_bytes=64)
        b_codes = keep.tile([P, CHUNKS, KINDS, BANK], U32, name="b_codes", align_bytes=64)
        b_scales = keep.tile([P, CHUNKS, KINDS, BANK], U8, name="b_scales", align_bytes=64)

        def load_b(chunk):
            cols = slice(chunk * CHUNK_COLS, (chunk + 1) * CHUNK_COLS)
            nc.sync.dma_start(out=b_raw[:, chunk], in_=wqb_by_partition[:, :, cols])

        def load_a(g):
            rows = Wqa[g * K_PASS : (g + 1) * K_PASS, :]
            nc.sync.dma_start(
                out=a_raw[:, g].rearrange("p t n -> p (t n)"),
                in_=rows.rearrange("(p t) n -> p (t n)", p=P, t=PACK),
            )

        def load_x(i):
            x_raw[i] = arrivals.tile([P, D_MODEL], BF16, name="x_raw", tag="x_raw")
            nc.sync.dma_start(out=x_raw[i][:], in_=x_rows[i * P : (i + 1) * P, :])

        tiles_per_chunk = TOKEN_TILES // CHUNKS
        for i in range(TOKEN_TILES):
            load_x(i)
            if i == 0:
                for g in range(D_PASSES):
                    load_a(g)
            if i % tiles_per_chunk == tiles_per_chunk - 1:
                load_b(i // tiles_per_chunk)

        sin_half, cos_half = build_half_angle_sines(nc, keep)
        identity = keep.tile([P, P], F32, name="identity")
        make_identity(nc, identity[:])

        b_grouped = {}

        def regroup_b(copy, chunk, kind, first_head, heads):
            if first_head == 0:
                b_grouped[(chunk, kind)] = stage.tile(
                    [P, BANK, PACK], BF16, name="b_grouped", tag="b_grouped", align_bytes=64
                )
            some = slice(first_head, first_head + heads)
            grouped = b_grouped[(chunk, kind)]
            if kind == PLAIN_KIND:
                copy(
                    out=grouped[:].rearrange("p (h c i) t -> p h c t i", h=CHUNK_HEADS, i=4)[:, some],
                    in_=b_raw[:, chunk].rearrange(
                        "p t (h k c i) -> p k h c t i", h=CHUNK_HEADS, k=KINDS, i=4
                    )[:, PLAIN_KIND, some],
                )
            else:
                for block in range(2):
                    copy(
                        out=grouped[:].rearrange(
                            "p (b h c i) t -> p b h c t i", b=2, h=CHUNK_HEADS, i=4
                        )[:, block, some],
                        in_=b_raw[:, chunk].rearrange(
                            "p t (h k c i e) -> p k e h c t i", h=CHUNK_HEADS, k=KINDS, i=4, e=2
                        )[:, ROTARY_KIND, 1 - block, some],
                    )

        quantised_chunks = set()

        def quantise_b(chunk, kind):
            if kind == PLAIN_KIND:
                quantised_chunks.add(chunk)
            nc.vector.quantize_mx(
                out=b_codes[:, chunk, kind, :].bitcast(FP8X4),
                scales=b_scales[:, chunk, kind, :],
                in_=b_grouped[(chunk, kind)][:].rearrange("p n t -> p (n t)"),
            )

        def prepare_b(chunk):
            pieces = []
            for kind in (ROTARY_KIND, PLAIN_KIND):
                if (chunk, kind) in SCALAR_KINDS:
                    for head in range(CHUNK_HEADS):
                        pieces.append(lambda kind=kind, head=head: regroup_b(nc.scalar.copy, chunk, kind, head, 1))
                else:
                    pieces.append(lambda kind=kind: regroup_b(nc.vector.tensor_copy, chunk, kind, 0, CHUNK_HEADS))
            for kind in (ROTARY_KIND, PLAIN_KIND):
                pieces.append(lambda kind=kind: quantise_b(chunk, kind))
            return pieces

        a_grouped = {}

        def regroup_a(g):
            a_grouped[g] = stage.tile([P, Q_RANK, PACK], BF16, name="a_grouped", tag="a_grouped", bufs=D_PASSES, align_bytes=64)
            grouped = a_grouped[g][:].rearrange("p (s c i) t -> p s c t i", s=RANK_TILES, i=4)
            raw = a_raw[:, g].rearrange("p t (c i s) -> p s c t i", s=RANK_TILES, i=4)
            if g in SCALAR_PASSES:
                for s in range(RANK_TILES):
                    nc.scalar.copy(out=grouped[:, s], in_=raw[:, s])
            else:
                nc.vector.tensor_copy(out=grouped, in_=raw)

        def quantise_a(g):
            nc.vector.quantize_mx(
                out=a_codes[:, g, :].bitcast(FP8X4),
                scales=a_scales[:, g, :],
                in_=a_grouped[g][:].rearrange("p n t -> p (n t)"),
            )

        x_grouped = {}

        def turn_x(i):
            x_words = x_raw[i][:].bitcast(F32)
            x_grouped[i] = stage.tile(
                [P, D_PASSES * P * PACK], BF16, name="x_grouped", tag="x_grouped", align_bytes=64
            )
            grouped_words = x_grouped[i][:].bitcast(F32).rearrange("p (g r u) -> p g r u", g=D_PASSES, r=P, u=2)
            passes_per_bank = 2
            for first_pass in range(0, D_PASSES, passes_per_bank):
                turned = psum.tile([P, passes_per_bank * 2, P], F32, name="turned", tag="bank")
                for c in range(passes_per_bank * 2):
                    first_word = (first_pass + c // 2) * 2 * P + c % 2
                    nc.tensor.transpose(
                        turned[:, c, :], x_words[:, first_word : first_word - c % 2 + 2 * P : 2], identity[:]
                    )
                nc.scalar.copy(
                    out=grouped_words[:, first_pass : first_pass + passes_per_bank],
                    in_=turned[:].rearrange("p (g u) r -> p g r u", u=2),
                )

        def quantise_x(i):
            nc.vector.quantize_mx(
                out=x_codes[:, i].rearrange("p g r -> p (g r)").bitcast(FP8X4),
                scales=x_scales[:, i].rearrange("p g r -> p (g r)"),
                in_=x_grouped[i][:],
            )

        cq_grouped = {}

        def first_product(i):
            cq_bank = psum.tile([P, RANK_TILES, P], F32, name="cq_bank", tag="bank")
            for t in range(RANK_TILES):
                for g in range(D_PASSES):
                    nc.tensor.matmul_mx(
                        out=cq_bank[:, t, :],
                        lhsT=a_codes[:, g, t * P : (t + 1) * P].bitcast(FP8X4),
                        lhsT_scale=a_scales[:, g, t * P : (t + 1) * P],
                        rhs=x_codes[:, i, g, :].bitcast(FP8X4),
                        rhs_scale=x_scales[:, i, g, :],
                        start=(g == 0),
                        stop=(g == D_PASSES - 1),
                    )
            cq_grouped[i] = stage.tile([P, P, PACK], BF16, name="cq_grouped", tag="cq_grouped", align_bytes=64)
            nc.scalar.copy(out=cq_grouped[i][:], in_=cq_bank[:].rearrange("p t r -> p r t"))

        def quantise_cq(i):
            nc.vector.quantize_mx(
                out=cq_codes[:, i, :].bitcast(FP8X4),
                scales=cq_scales[:, i, :],
                in_=cq_grouped[i][:].rearrange("p r t -> p (r t)"),
            )

        def second_pass(i, bank, chunk, kind, cols, start, stop):
            nc.tensor.matmul_mx(
                out=bank,
                lhsT=cq_codes[:, i, :].bitcast(FP8X4),
                lhsT_scale=cq_scales[:, i, :],
                rhs=b_codes[:, chunk, kind, cols].bitcast(FP8X4),
                rhs_scale=b_scales[:, chunk, kind, cols],
                start=start,
                stop=stop,
            )

        unfinished = []

        def second_product(i, chunk):
            w_then_u = psum.tile([P, 2, CHUNK_PAIRS], F32, name="w_then_u", tag="bank")
            second_pass(i, w_then_u[:].rearrange("p b n -> p (b n)"), chunk, ROTARY_KIND, slice(0, BANK), True, True)
            u_plus_w = psum.tile([P, CHUNK_PAIRS], F32, name="u_plus_w", tag="bank")
            second_pass(i, u_plus_w[:], chunk, ROTARY_KIND, slice(0, CHUNK_PAIRS), True, False)
            second_pass(i, u_plus_w[:], chunk, ROTARY_KIND, slice(CHUNK_PAIRS, BANK), False, True)
            plain = psum.tile([P, BANK], F32, name="plain", tag="bank")
            second_pass(i, plain[:], chunk, PLAIN_KIND, slice(0, BANK), True, True)

            half = i % SEQ_HALVES
            heads = results.tile([P, CHUNK_HEADS, HEAD], F32, name="heads")
            nc.vector.tensor_tensor(
                out=heads[:, :, PLAIN:HEAD].rearrange("p h (j e) -> p h j e", e=2),
                in0=w_then_u[:].rearrange("p b (h j) -> p h j b", h=CHUNK_HEADS),
                in1=mixed[:, half].unsqueeze(1).to_broadcast([P, CHUNK_HEADS, PAIRS, 2]),
                op=ALU.mult,
            )
            shared = results.tile([P, CHUNK_HEADS, PAIRS], F32, name="shared")
            nc.vector.tensor_tensor(
                out=shared[:],
                in0=u_plus_w[:].rearrange("p (h j) -> p h j", h=CHUNK_HEADS),
                in1=cosine[:, half].unsqueeze(1).to_broadcast([P, CHUNK_HEADS, PAIRS]),
                op=ALU.mult,
            )
            nc.scalar.copy(
                out=heads[:, :, 0:PLAIN], in_=plain[:].rearrange("p (h f) -> p h f", h=CHUNK_HEADS)
            )
            if unfinished:
                add_and_store(*unfinished[-1])
            unfinished.append((i, chunk, heads, shared))

        def add_and_store(i, chunk, heads, shared):
            left = TOKEN_TILES * CHUNKS - len(unfinished)
            adder = nc.gpsimd if len(unfinished) % VECTOR_ADDS > 0 and left > 1 else nc.vector
            share = CHUNK_HEADS if left else LAST_HEADS
            for first in range(0, CHUNK_HEADS, share):
                some = slice(first, first + share)
                rotated = heads[:, some, PLAIN:HEAD].rearrange("p h (j e) -> p h j e", e=2)
                adder.tensor_tensor(
                    out=rotated,
                    in0=rotated,
                    in1=shared[:, some].unsqueeze(3).to_broadcast([P, share, PAIRS, 2]),
                    op=ALU.add,
                )
                first_col = chunk * CHUNK_COLS + first * HEAD
                nc.sync.dma_start(
                    out=out_rows[i * P : (i + 1) * P, first_col : first_col + share * HEAD],
                    in_=heads[:, some].rearrange("p h f -> p (h f)"),
                )

        turn_x(0)
        for g in range(D_PASSES):
            regroup_a(g)
            if g == 0:
                quantise_x(0)
        turn_x(1)
        for g in range(D_PASSES):
            quantise_a(g)
            if g == 0:
                cosine, mixed = build_rotation_tables(nc, keep, sin_half, cos_half)
        quantise_x(1)
        regroup_b(nc.vector.tensor_copy, 0, ROTARY_KIND, 0, CHUNK_HEADS)
        for head in range(CHUNK_HEADS):
            regroup_b(nc.scalar.copy, 0, PLAIN_KIND, head, 1)
        quantise_b(0, ROTARY_KIND)

        units = sorted(((i, c) for i in range(TOKEN_TILES) for c in range(CHUNKS)), key=lambda u: (u[0] + CHUNK_LAG * u[1], u[1]))
        pieces = [piece for chunk in range(1, CHUNKS) for piece in prepare_b(chunk)]
        for step in range(TOKEN_TILES * CHUNKS // FULL_RATE + 2 * len(RAMP)):
            if step + TURN_AHEAD < TOKEN_TILES:
                turn_x(step + TURN_AHEAD)
            if step < TOKEN_TILES:
                first_product(step)
            if step == 0:
                quantise_b(0, PLAIN_KIND)
            for unused in range(RAMP[step] if step < len(RAMP) else FULL_RATE):
                ready = [unit for unit in units if unit[0] < step and unit[1] in quantised_chunks]
                if ready:
                    i, chunk = ready[0]
                    units.remove(ready[0])
                    second_product(i, chunk)
            if step < TOKEN_TILES:
                quantise_cq(step)
            for unused in range(PIECES_RAMP[step] if step < len(PIECES_RAMP) else PIECES):
                if pieces:
                    pieces.pop(0)()
            if step + TURN_AHEAD < TOKEN_TILES:
                quantise_x(step + TURN_AHEAD)
        assert not units and not pieces
        add_and_store(*unfinished[-1])
